import numpy as np
import ml_dtypes


def mxq(x, axis, fmt="e4m3"):
    dtype, down = {"e4m3": (ml_dtypes.float8_e4m3fn, 7), "e5m2": (ml_dtypes.float8_e5m2, 14)}[fmt]
    v = np.moveaxis(np.asarray(x, np.float32).astype(ml_dtypes.bfloat16).astype(np.float64), axis, -1)
    blocks = v.reshape(v.shape[:-1] + (-1, 32))
    amax = np.abs(blocks).max(-1, keepdims=True)
    byte = np.maximum(np.where(amax > 0, np.frexp(amax)[1] - 1 + 127, 0) - down, 1)
    scale = np.exp2(byte - 127.0)
    codes = (blocks / scale).astype(np.float32).astype(dtype).astype(np.float64)
    return np.moveaxis((codes * scale).reshape(v.shape), -1, axis)


WIDE = False


def mx_kscale(k):
    if not WIDE:
        return np.ones(k)
    levels = np.array([10, -10, 5, -5, 0])
    if k % 512:
        return np.exp2(np.random.permutation(np.resize(levels, k // 32))).repeat(32)
    a = np.empty((k // 512, 16))
    for p in range(k // 512):
        a[p, :8] = np.random.permutation(np.resize(levels, 8))
        for g in range(8):
            far = levels[np.abs(levels - a[p, g]) >= 10]
            a[p, g + 8] = far[np.random.randint(len(far))]
    return np.exp2(a.ravel()).repeat(32)


BF16 = ml_dtypes.bfloat16


def bf(x):
    return np.asarray(x, np.float32).astype(BF16)


def f64(x):
    return np.asarray(x).astype(np.float64)


E2M1 = np.array([0.0, 0.5, 1.0, 1.5, 2.0, 3.0, 4.0, 6.0, -0.0, -0.5, -1.0, -1.5, -2.0, -3.0, -4.0, -6.0])


def pack_weight(w, fmt):
    k, n = w.shape
    w = f64(bf(w)).reshape(k // 32, 32, n)
    amax = np.abs(w).max(1)
    if fmt == "e4m3":
        byte = np.frexp(amax)[1] - 1 + 127 - 7
    else:
        mant, ex = np.frexp(amax / 6.0)
        byte = np.where(mant > 0.5, ex, ex - 1) + 127
    byte = np.clip(np.where(amax > 0, byte, 1), 1, 254)
    scaled = (w * np.exp2(127.0 - byte)[:, None, :]).reshape(k, n).astype(np.float32)
    by_word = np.ascontiguousarray(scaled.reshape(k // 512, 128, 4, n).transpose(0, 1, 3, 2))
    if fmt == "e4m3":
        words = by_word.astype(ml_dtypes.float8_e4m3fn).view(np.uint8)
    else:
        c = by_word.astype(ml_dtypes.float4_e2m1fn).view(np.uint8) & 0xF
        words = c[..., 0::2] | (c[..., 1::2] << 4)
    return np.ascontiguousarray(words), np.ascontiguousarray(byte.astype(np.uint8).reshape(k // 512, 16, n))


def unpack_weight(words, scales, fmt):
    g, p, n, _ = words.shape
    if fmt == "e4m3":
        vals = np.ascontiguousarray(words).view(ml_dtypes.float8_e4m3fn).astype(np.float64)
    else:
        nib = np.empty((g, p, n, 4), np.uint8)
        nib[..., 0::2] = words & 0xF
        nib[..., 1::2] = words >> 4
        vals = E2M1[nib]
    vals = vals * np.repeat(np.exp2(scales.astype(np.float64) - 127.0), 8, axis=1)[..., None]
    return vals.transpose(0, 1, 3, 2).reshape(g * 512, n)
def pack4(w):
    words, scales = pack_weight(w, "e2m1")
    return words.reshape(words.shape[0], 128, -1), scales


def unpack4(words, scales):
    return unpack_weight(words.reshape(words.shape[0], 128, -1, 2), scales, "e2m1")


B, S, D, H, NOPE, ROPE, VD, KV_RANK, Q_RANK = 2, 2048, 1024, 2, 64, 128, 64, 512, 1536
EPS = 1e-6
THETA = 10000.0
LAT = 0.005
PE = 0.1
HALF = ROPE // 2


def rmsnorm(v, g):
    return v * (1.0 / np.sqrt(np.mean(v * v, axis=-1, keepdims=True) + EPS)) * g


def rope(v):
    inv = 1.0 / THETA ** (np.arange(HALF) / HALF)
    ang = np.arange(S)[:, None] * inv[None, :]
    cos = np.cos(ang)[None, :, None, :]
    sin = np.sin(ang)[None, :, None, :]
    v1, v2 = v[..., :HALF], v[..., HALF:]
    return np.concatenate([v1 * cos - v2 * sin, v2 * cos + v1 * sin], axis=-1)


def draw0():
    s, t = mx_kscale(D), mx_kscale(KV_RANK)
    col = np.concatenate([np.full(KV_RANK, LAT), np.full(ROPE, PE)]) / np.sqrt(D)
    x = bf(np.random.standard_normal((B, S, D)) * s)
    w_dkv_words, w_dkv_scales = pack4(np.random.standard_normal((D, KV_RANK + ROPE)) * col / s[:, None])
    kv_a_norm = bf((1.0 + 0.1 * np.random.standard_normal(KV_RANK)) * t)
    w_ukv_words, w_ukv_scales = pack4(np.random.standard_normal((KV_RANK, H * (NOPE + VD))) / np.sqrt(KV_RANK) / t[:, None])
    return {"x": x,
            "w_dkv_words": w_dkv_words,
            "w_dkv_scales": w_dkv_scales,
            "kv_a_norm": kv_a_norm,
            "w_ukv_words": w_ukv_words,
            "w_ukv_scales": w_ukv_scales}


def core(x, w_dkv_words, w_dkv_scales, kv_a_norm, w_ukv_words, w_ukv_scales):
    xq = mxq(f64(x), 2, "e4m3")
    wd = unpack4(w_dkv_words, w_dkv_scales)
    c_kv = xq @ wd[:, :KV_RANK]
    k_pe = xq @ wd[:, KV_RANK:]
    h = rmsnorm(c_kv, f64(kv_a_norm))
    kv = (mxq(h, 2, "e4m3") @ unpack4(w_ukv_words, w_ukv_scales)).reshape(B, S, H, NOPE + VD)
    k_nope, v = kv[..., :NOPE], kv[..., NOPE:]
    k_pe = rope(k_pe[:, :, None, :])
    kf = np.concatenate([k_nope, np.broadcast_to(k_pe, (B, S, H, ROPE))], axis=-1)
    return kf, v


def e4m3fn_bytes(y):
    return np.clip(np.asarray(y, np.float64), -448.0, 448.0).astype(np.float32).astype(ml_dtypes.float8_e4m3fn).view(np.uint8)


def e4m3fn_values(b):
    return np.asarray(b, np.uint8).view(ml_dtypes.float8_e4m3fn).astype(np.float64)


def setup_inputs():
    d = draw0()
    x0 = np.asarray(d['x']).astype(np.float64)
    s = (np.max(np.abs(x0), axis=(0, 1), keepdims=True) / 448.0).astype(np.float32)
    out = {}
    for k, v in d.items():
        if k == 'x':
            out['x_bytes'] = e4m3fn_bytes(x0 / s.astype(np.float64))
            out['x_scale'] = s
        else:
            out[k] = v
    return out


def reference(x_bytes, x_scale, w_dkv_words, w_dkv_scales, kv_a_norm, w_ukv_words, w_ukv_scales):
    return core(e4m3fn_values(x_bytes) * x_scale.astype(np.float64), w_dkv_words, w_dkv_scales, kv_a_norm, w_ukv_words, w_ukv_scales)

@@ -1,0 +1,323 @@
+import math
+from contextlib import ExitStack
+
+import concourse.mybir as mybir
+from concourse.masks import make_identity
+
+F32 = mybir.dt.float32
+BF16 = mybir.dt.bfloat16
+I32 = mybir.dt.int32
+U32 = mybir.dt.uint32
+U8 = mybir.dt.uint8
+FP8 = mybir.dt.float8_e4m3fn
+E4M3X4 = mybir.dt.float8_e4m3fn_x4
+E2M1X4 = mybir.dt.float4_e2m1fn_x4
+ALU = mybir.AluOpType
+ACT = mybir.ActivationFunctionType
+
+B, S, D, KV, ROPE, HEADS, FEAT = 2, 2048, 1024, 512, 128, 2, 64
+TOK = B * S
+N1 = KV + ROPE
+N2 = HEADS * 2 * FEAT
+P = 128
+EPS = 1e-6
+THETA = 10000.0
+FLOPS = 2 * TOK * D * N1 + 2 * TOK * KV * N2
+
+J = 2
+PAIR = P * J
+NPAIR = TOK // PAIR
+PER_B = S // PAIR
+G1 = D // 512
+CHUNKS = 4
+
+
+def tile_multiheadlatentattention_pb_t_w4_kernel(
+    tc, x_bytes, x_scale, w_dkv_words, w_dkv_scales, kv_a_norm, w_ukv_words, w_ukv_scales, out_0, out_1
+):
+    nc = tc.nc
+    pair_of = [(n % B) * PER_B + n // B for n in range(NPAIR)]
+
+    xb_hbm = x_bytes.rearrange("b s k -> (b s) k").rearrange("(n p j) k -> n p (j k)", p=P, j=J)
+    kf_hbm = out_0.rearrange("b s h c -> (b s) (h c)").rearrange("(n p j) c -> n p j c", p=P, j=J)
+    v_hbm = out_1.rearrange("b s h c -> (b s) (h c)").rearrange("(n p j) c -> n p (j c)", p=P, j=J)
+
+    with ExitStack() as ctx:
+        keep = ctx.enter_context(tc.tile_pool(name="keep", bufs=1))
+        work = ctx.enter_context(tc.tile_pool(name="work", bufs=3))
+        psum = ctx.enter_context(tc.psum_pool(name="psum", bufs=1))
+        ctx.enter_context(tc.manual_schedule())
+
+        xb = keep.tile([P, NPAIR, J * D], U8, name="xb", align_bytes=64)
+        xs = keep.tile([P, G1, 4], F32, name="xs", align_bytes=64)
+        wd = keep.tile([P, G1, 2 * N1], U8, name="wd", align_bytes=64)
+        wds = keep.tile([P, G1, N1], U8, name="wds", align_bytes=64)
+        wu = keep.tile([P, 2 * N2], U8, name="wu", align_bytes=64)
+        wus = keep.tile([P, N2], U8, name="wus", align_bytes=64)
+        gain = keep.tile([P, KV], BF16, name="gain", align_bytes=64)
+        ident = keep.tile([P, P], F32, name="ident", align_bytes=64)
+        eps = keep.tile([P, 1], F32, name="eps")
+        one = keep.tile([P, 1], F32, name="one")
+        dummy = keep.tile([P, 1], F32, name="dummy")
+        pos = keep.tile([P, PER_B * J], F32, name="pos")
+        theta = keep.tile([P, FEAT], F32, name="theta")
+        turns = keep.tile([P, PER_B * J, FEAT], F32, name="turns")
+        whole = keep.tile([P, PER_B * J, FEAT], I32, name="whole")
+        frac = keep.tile([P, PER_B * J, FEAT], F32, name="frac")
+        half = keep.tile([P, PER_B * J, FEAT], F32, name="half")
+        square = keep.tile([P, PER_B * J, FEAT], F32, name="square")
+        sin = keep.tile([P, PER_B * J, FEAT], F32, name="sin")
+        cos = keep.tile([P, PER_B * J, FEAT], F32, name="cos")
+
+        nc.vector.memset(one[:], 1.0)
+        nc.vector.memset(wds[:].rearrange("p g n -> p (g n)").bitcast(I32), 0)
+        nc.vector.memset(wus[:].bitcast(I32), 0)
+        nc.scalar.activation(dummy[:], one[:], ACT.Sin)
+
+        def load_x(n):
+            nc.sync.dma_start(out=xb[:, n, :], in_=xb_hbm[pair_of[n]])
+
+        load_x(0)
+        nc.sync.dma_start(
+            out=xs[:], in_=x_scale.rearrange("a b (g p t) -> p (a b g) t", p=P, t=4)
+        )
+        load_x(1)
+        nc.sync.dma_start(
+            out=wd[:].bitcast(I32),
+            in_=w_dkv_words.rearrange("g p n -> p g n").bitcast(I32),
+        )
+        for q in range(4):
+            nc.sync.dma_start(
+                out=wds[32 * q : 32 * q + 4].bitcast(I32),
+                in_=w_dkv_scales[:, 4 * q : 4 * q + 4, :].rearrange("g q n -> q g n").bitcast(I32),
+            )
+        for q in range(4):
+            nc.sync.dma_start(
+                out=wus[32 * q : 32 * q + 4].bitcast(I32),
+                in_=w_ukv_scales[0, 4 * q : 4 * q + 4, :].bitcast(I32),
+            )
+        nc.sync.dma_start(out=gain[:], in_=kv_a_norm.partition_broadcast(P))
+        load_x(2)
+        nc.sync.dma_start(out=wu[:].bitcast(I32), in_=w_ukv_words[0].bitcast(I32))
+        for n in range(3, NPAIR):
+            load_x(n)
+
+        make_identity(nc, ident[:])
+        nc.gpsimd.iota(
+            pos[:], [[PAIR, PER_B], [1, J]], base=0, channel_multiplier=J, allow_small_or_imprecise_dtypes=True
+        )
+        nc.vector.tensor_scalar(theta[:, 0:1], one[:], 1.0 / (2.0 * math.pi), None, ALU.mult)
+        nc.vector.tensor_scalar(eps[:], one[:], -1.0, EPS, ALU.add, ALU.add)
+        width = 1
+        while width < FEAT:
+            nc.vector.tensor_scalar(
+                theta[:, width : 2 * width], theta[:, 0:width], THETA ** (-width / FEAT), None, ALU.mult
+            )
+            width *= 2
+        rows = PER_B * J // CHUNKS
+        for c in range(CHUNKS):
+            sl = slice(c * rows, (c + 1) * rows)
+            nc.gpsimd.tensor_tensor(
+                turns[:, sl],
+                pos[:, sl].unsqueeze(2).to_broadcast([P, rows, FEAT]),
+                theta[:].unsqueeze(1).to_broadcast([P, rows, FEAT]),
+                ALU.mult,
+            )
+            nc.vector.tensor_copy(whole[:, sl], turns[:, sl])
+            nc.vector.tensor_tensor(frac[:, sl], turns[:, sl], whole[:, sl], ALU.subtract)
+
+        def trig_scalar(c):
+            sl = slice(c * rows, (c + 1) * rows)
+            nc.scalar.activation(half[:, sl], frac[:, sl], ACT.Sin, scale=math.pi)
+            nc.scalar.activation(sin[:, sl], frac[:, sl], ACT.Sin, scale=2.0 * math.pi)
+
+        def trig_gpsimd(c):
+            sl = slice(c * rows, (c + 1) * rows)
+            nc.gpsimd.tensor_tensor(square[:, sl], half[:, sl], half[:, sl], ALU.mult)
+            nc.gpsimd.tensor_scalar(cos[:, sl], square[:, sl], -2.0, 1.0, ALU.mult, ALU.add)
+
+        live = {}
+
+        def cast(n):
+            xw = work.tile([P, J, D], BF16, name="xw", align_bytes=64)
+            for j in range(J):
+                nc.scalar.copy(xw[:, j, :], xb[:, n, j * D : (j + 1) * D].bitcast(FP8))
+            live["xw", n] = xw
+
+        def transpose_x(n):
+            words = live.pop(("xw", n))[:].rearrange("p j k -> p (j k)").bitcast(F32)
+            for j in range(J):
+                px = psum.tile([P, 2, G1, P], F32, name="px", bufs=3)
+                for u in range(2):
+                    for g in range(G1):
+                        lo = j * D // 2 + g * 256
+                        nc.tensor.transpose(px[:, u, g, :], words[:, lo + u : lo + 256 : 2], ident[:])
+                live["px", n, j] = px
+
+        def scale_x(n):
+            xg = work.tile([P, J, D // 2, 2], BF16, name="xg", align_bytes=64)
+            for j in range(J):
+                px = live.pop(("px", n, j))
+                nc.vector.tensor_tensor(
+                    xg[:, j].rearrange("p (g r u) e -> p g r u e", g=G1, u=2),
+                    px[:].rearrange("p u g r -> p (u g r)").bitcast(BF16).rearrange(
+                        "p (u g r e) -> p g r u e", u=2, g=G1, e=2
+                    ),
+                    xs[:].rearrange("p g (u e) -> p g u e", u=2).unsqueeze(2).to_broadcast([P, G1, P, 2, 2]),
+                    ALU.mult,
+                )
+            live["xg", n] = xg
+
+        def quantize_x(n):
+            xg = live.pop(("xg", n))
+            xc = work.tile([P, J * G1 * P], U32, name="xc", align_bytes=64)
+            xcs = work.tile([P, J * G1 * P], U8, name="xcs", align_bytes=64)
+            nc.vector.quantize_mx(
+                out=xc[:].bitcast(E4M3X4), scales=xcs[:], in_=xg[:].rearrange("p j n e -> p (j n e)")
+            )
+            live["xc", n] = (xc, xcs)
+
+        def matmul_x(n):
+            xc, xcs = live.pop(("xc", n))
+            r = psum.tile([P, J, ROPE], F32, name="r")
+            for j in range(J):
+                c = psum.tile([P, KV], F32, name="c", bufs=2)
+                for out, lo, hi in ((c[:], 0, KV), (r[:, j, :], KV, N1)):
+                    for g in range(G1):
+                        cols = slice((j * G1 + g) * P, (j * G1 + g + 1) * P)
+                        nc.tensor.matmul_mx(
+                            out=out,
+                            lhsT=xc[:, cols].bitcast(E4M3X4),
+                            lhsT_scale=xcs[:, cols],
+                            rhs=wd[:, g, 2 * lo : 2 * hi].bitcast(E2M1X4),
+                            rhs_scale=wds[:, g, lo:hi],
+                            start=(g == 0),
+                            stop=(g == G1 - 1),
+                        )
+                live["c", n, j] = c
+            live["r", n] = r
+
+        def norm(n):
+            ss = work.tile([P, J], F32, name="ss")
+            rstd = work.tile([P, J], F32, name="rstd")
+            for j in range(J):
+                junk = work.tile([P, KV], BF16, name="junk")
+                nc.scalar.activation(junk[:], live["c", n, j][:], ACT.Square, accum_out=ss[:, j : j + 1])
+            nc.scalar.activation(rstd[:], ss[:], ACT.Abs_reciprocal_sqrt, bias=eps[:], scale=1.0 / KV)
+            live["rstd", n] = rstd
+
+        def make_h(n):
+            rstd = live.pop(("rstd", n))
+            h = work.tile([P, J, KV], BF16, name="h", align_bytes=64)
+            for j in range(J):
+                c = live.pop(("c", n, j))
+                nc.vector.scalar_tensor_tensor(h[:, j, :], c[:], rstd[:, j : j + 1], gain[:], ALU.mult, ALU.mult)
+            live["h", n] = h
+
+        def transpose_h(n):
+            words = live.pop(("h", n))[:].rearrange("p j k -> p (j k)").bitcast(F32)
+            ph = psum.tile([P, 2, J, P], F32, name="ph")
+            for j in range(J):
+                for u in range(2):
+                    nc.tensor.transpose(ph[:, u, j, :], words[:, 256 * j + u : 256 * (j + 1) : 2], ident[:])
+            live["ph", n] = ph
+
+        def copy_h(n):
+            hg = work.tile([P, J * P, 4], BF16, name="hg", align_bytes=64)
+            nc.scalar.copy(
+                hg[:].rearrange("p r t -> p (r t)").bitcast(F32).rearrange("p (r u) -> p r u", u=2),
+                live.pop(("ph", n))[:].rearrange("p u j r -> p (j r) u"),
+            )
+            live["hg", n] = hg
+
+        def quantize_h(n):
+            hc = work.tile([P, J * P], U32, name="hc", align_bytes=64)
+            hcs = work.tile([P, J * P], U8, name="hcs", align_bytes=64)
+            nc.vector.quantize_mx(
+                out=hc[:].bitcast(E4M3X4), scales=hcs[:], in_=live.pop(("hg", n))[:].rearrange("p r t -> p (r t)")
+            )
+            live["hc", n] = (hc, hcs)
+
+        def matmul_h(n):
+            hc, hcs = live.pop(("hc", n))
+            kv = psum.tile([P, J, N2], F32, name="kv")
+            for j in range(J):
+                cols = slice(j * P, (j + 1) * P)
+                nc.tensor.matmul_mx(
+                    out=kv[:, j, :],
+                    lhsT=hc[:, cols].bitcast(E4M3X4),
+                    lhsT_scale=hcs[:, cols],
+                    rhs=wu[:].bitcast(E2M1X4),
+                    rhs_scale=wus[:],
+                    start=True,
+                    stop=True,
+                )
+            live["kv", n] = kv
+
+        def kf_tile(n):
+            if ("kf", n) not in live:
+                live["kf", n] = work.tile([P, J, 4, FEAT], F32, name="kf", bufs=4)
+            return live["kf", n]
+
+        def copy_r(n):
+            rs = work.tile([P, J, 2, FEAT], F32, name="rs")
+            nc.scalar.copy(rs[:].rearrange("p j d i -> p j (d i)"), live.pop(("r", n))[:])
+            live["rs", n] = rs
+
+        def rope(n):
+            kf = kf_tile(n)
+            rs = live.pop(("rs", n))
+            at = slice(n // B * J, (n // B + 1) * J)
+            by_cos = work.tile([P, J, 2, FEAT], F32, name="by_cos")
+            by_sin = work.tile([P, J, 2, FEAT], F32, name="by_sin")
+            shape = [P, J, 2, FEAT]
+            nc.gpsimd.tensor_tensor(by_cos[:], rs[:], cos[:, at].unsqueeze(2).to_broadcast(shape), ALU.mult)
+            nc.gpsimd.tensor_tensor(by_sin[:], rs[:], sin[:, at].unsqueeze(2).to_broadcast(shape), ALU.mult)
+            nc.gpsimd.tensor_tensor(kf[:, :, 1, :], by_cos[:, :, 0, :], by_sin[:, :, 1, :], ALU.subtract)
+            nc.gpsimd.tensor_tensor(kf[:, :, 2, :], by_cos[:, :, 1, :], by_sin[:, :, 0, :], ALU.add)
+
+        def copy_kv(n):
+            kf = kf_tile(n)
+            v = work.tile([P, J, HEADS, FEAT], F32, name="v")
+            kv = live.pop(("kv", n))[:].rearrange("p j (h d i) -> p j h d i", h=HEADS, d=2)
+            nc.scalar.copy(kf[:, :, 0:4:3, :], kv[:, :, :, 0, :])
+            nc.scalar.copy(v[:], kv[:, :, :, 1, :])
+            live["v", n] = v
+
+        def store(n):
+            at = pair_of[n]
+            kf = live.pop(("kf", n))[:].rearrange("p j b i -> p j (b i)")
+            v = live.pop(("v", n))
+            nc.sync.dma_start(out=kf_hbm[at, :, :, 0:256], in_=kf)
+            nc.sync.dma_start(out=kf_hbm[at, :, :, 256:384], in_=kf[:, :, 64:192])
+            nc.sync.dma_start(out=v_hbm[at], in_=v[:].rearrange("p j h i -> p (j h i)"))
+
+        def run(stage, n):
+            if 0 <= n < NPAIR:
+                stage(n)
+
+        cast(0)
+        trig_scalar(0)
+        cast(1)
+        for c in range(1, CHUNKS):
+            trig_scalar(c)
+        for c in range(CHUNKS):
+            trig_gpsimd(c)
+        transpose_x(0)
+
+        for s in range(0, NPAIR + 3):
+            run(copy_h, s - 2)
+            run(matmul_x, s - 1)
+            run(norm, s - 1)
+            run(matmul_h, s - 3)
+            run(copy_kv, s - 3)
+            run(scale_x, s)
+            run(make_h, s - 1)
+            run(quantize_x, s)
+            run(quantize_h, s - 2)
+            run(copy_r, s - 1)
+            run(rope, s - 1)
+            run(cast, s + 2)
+            run(transpose_x, s + 1)
+            run(transpose_h, s - 1)
+            run(store, s - 3)

@@ -30,6 +30,8 @@ NPAIR = TOK // PAIR
 PER_B = S // PAIR
 G1 = D // 512
 CHUNKS = 4
+NTILE = NPAIR * J
+ON_VECTOR = 192
 
 
 def tile_multiheadlatentattention_pb_t_w4_kernel(
@@ -40,7 +42,7 @@ def tile_multiheadlatentattention_pb_t_w4_kernel(
 
     xb_hbm = x_bytes.rearrange("b s k -> (b s) k").rearrange("(n p j) k -> n p (j k)", p=P, j=J)
     kf_hbm = out_0.rearrange("b s h c -> (b s) (h c)").rearrange("(n p j) c -> n p j c", p=P, j=J)
-    v_hbm = out_1.rearrange("b s h c -> (b s) (h c)").rearrange("(n p j) c -> n p (j c)", p=P, j=J)
+    v_hbm = out_1.rearrange("b s h c -> (b s) (h c)").rearrange("(n p j) c -> n p j c", p=P, j=J)
 
     with ExitStack() as ctx:
         keep = ctx.enter_context(tc.tile_pool(name="keep", bufs=1))
@@ -77,7 +79,9 @@ def tile_multiheadlatentattention_pb_t_w4_kernel(
         def load_x(n):
             nc.sync.dma_start(out=xb[:, n, :], in_=xb_hbm[pair_of[n]])
 
-        load_x(0)
+        for j in range(J):
+            cols = slice(j * D, (j + 1) * D)
+            nc.sync.dma_start(out=xb[:, 0, cols], in_=xb_hbm[pair_of[0], :, cols])
         nc.sync.dma_start(
             out=xs[:], in_=x_scale.rearrange("a b (g p t) -> p (a b g) t", p=P, t=4)
         )
@@ -139,185 +143,185 @@ def tile_multiheadlatentattention_pb_t_w4_kernel(
         live = {}
 
         def cast(n):
-            xw = work.tile([P, J, D], BF16, name="xw", align_bytes=64)
-            for j in range(J):
-                nc.scalar.copy(xw[:, j, :], xb[:, n, j * D : (j + 1) * D].bitcast(FP8))
+            xw = work.tile([P, D], BF16, name="xw", bufs=7, align_bytes=64)
+            codes = xb[:, n // J, n % J * D : (n % J + 1) * D]
+            cut = D - ON_VECTOR
+            nc.scalar.copy(xw[:, :cut], codes[:, :cut].bitcast(FP8))
+            nc.vector.tensor_copy(xw[:, cut:], codes[:, cut:].bitcast(FP8))
             live["xw", n] = xw
 
         def transpose_x(n):
-            words = live.pop(("xw", n))[:].rearrange("p j k -> p (j k)").bitcast(F32)
-            for j in range(J):
-                px = psum.tile([P, 2, G1, P], F32, name="px", bufs=3)
-                for u in range(2):
-                    for g in range(G1):
-                        lo = j * D // 2 + g * 256
-                        nc.tensor.transpose(px[:, u, g, :], words[:, lo + u : lo + 256 : 2], ident[:])
-                live["px", n, j] = px
+            words = live.pop(("xw", n))[:].bitcast(F32)
+            px = psum.tile([P, 2, G1, P], F32, name="px", bufs=2)
+            for u in range(2):
+                for g in range(G1):
+                    nc.tensor.transpose(px[:, u, g, :], words[:, 256 * g + u : 256 * (g + 1) : 2], ident[:])
+            live["px", n] = px
 
         def scale_x(n):
-            xg = work.tile([P, J, D // 2, 2], BF16, name="xg", align_bytes=64)
-            for j in range(J):
-                px = live.pop(("px", n, j))
-                nc.vector.tensor_tensor(
-                    xg[:, j].rearrange("p (g r u) e -> p g r u e", g=G1, u=2),
-                    px[:].rearrange("p u g r -> p (u g r)").bitcast(BF16).rearrange(
-                        "p (u g r e) -> p g r u e", u=2, g=G1, e=2
-                    ),
-                    xs[:].rearrange("p g (u e) -> p g u e", u=2).unsqueeze(2).to_broadcast([P, G1, P, 2, 2]),
-                    ALU.mult,
-                )
+            xg = work.tile([P, D // 2, 2], BF16, name="xg", align_bytes=64)
+            nc.vector.tensor_tensor(
+                xg[:].rearrange("p (g r u) e -> p g r u e", g=G1, u=2),
+                live.pop(("px", n))[:].rearrange("p u g r -> p (u g r)").bitcast(BF16).rearrange(
+                    "p (u g r e) -> p g r u e", u=2, g=G1, e=2
+                ),
+                xs[:].rearrange("p g (u e) -> p g u e", u=2).unsqueeze(2).to_broadcast([P, G1, P, 2, 2]),
+                ALU.mult,
+            )
             live["xg", n] = xg
 
         def quantize_x(n):
-            xg = live.pop(("xg", n))
-            xc = work.tile([P, J * G1 * P], U32, name="xc", align_bytes=64)
-            xcs = work.tile([P, J * G1 * P], U8, name="xcs", align_bytes=64)
+            xc = work.tile([P, G1 * P], U32, name="xc", bufs=5, align_bytes=64)
+            xcs = work.tile([P, G1 * P], U8, name="xcs", bufs=5, align_bytes=64)
             nc.vector.quantize_mx(
-                out=xc[:].bitcast(E4M3X4), scales=xcs[:], in_=xg[:].rearrange("p j n e -> p (j n e)")
+                out=xc[:].bitcast(E4M3X4), scales=xcs[:], in_=live.pop(("xg", n))[:].rearrange("p w e -> p (w e)")
             )
             live["xc", n] = (xc, xcs)
 
-        def matmul_x(n):
-            xc, xcs = live.pop(("xc", n))
-            r = psum.tile([P, J, ROPE], F32, name="r")
-            for j in range(J):
-                c = psum.tile([P, KV], F32, name="c", bufs=2)
-                for out, lo, hi in ((c[:], 0, KV), (r[:, j, :], KV, N1)):
-                    for g in range(G1):
-                        cols = slice((j * G1 + g) * P, (j * G1 + g + 1) * P)
-                        nc.tensor.matmul_mx(
-                            out=out,
-                            lhsT=xc[:, cols].bitcast(E4M3X4),
-                            lhsT_scale=xcs[:, cols],
-                            rhs=wd[:, g, 2 * lo : 2 * hi].bitcast(E2M1X4),
-                            rhs_scale=wds[:, g, lo:hi],
-                            start=(g == 0),
-                            stop=(g == G1 - 1),
-                        )
-                live["c", n, j] = c
-            live["r", n] = r
+        def matmul_x(out, n, lo, hi):
+            xc, xcs = live["xc", n]
+            for g in range(G1):
+                cols = slice(g * P, (g + 1) * P)
+                nc.tensor.matmul_mx(
+                    out=out,
+                    lhsT=xc[:, cols].bitcast(E4M3X4),
+                    lhsT_scale=xcs[:, cols],
+                    rhs=wd[:, g, 2 * lo : 2 * hi].bitcast(E2M1X4),
+                    rhs_scale=wds[:, g, lo:hi],
+                    start=(g == 0),
+                    stop=(g == G1 - 1),
+                )
 
-        def norm(n):
-            ss = work.tile([P, J], F32, name="ss")
-            rstd = work.tile([P, J], F32, name="rstd")
-            for j in range(J):
-                junk = work.tile([P, KV], BF16, name="junk")
-                nc.scalar.activation(junk[:], live["c", n, j][:], ACT.Square, accum_out=ss[:, j : j + 1])
-            nc.scalar.activation(rstd[:], ss[:], ACT.Abs_reciprocal_sqrt, bias=eps[:], scale=1.0 / KV)
+        def matmul_c(n):
+            c = psum.tile([P, KV], F32, name="c", bufs=3)
+            matmul_x(c[:], n, 0, KV)
+            live["c", n] = c
+
+        def matmul_r(n):
+            r = psum.tile([P, ROPE], F32, name="r")
+            matmul_x(r[:], n, KV, N1)
+            live["r", n] = r
+            live.pop(("xc", n))
+
+        def sum_squares(n):
+            ss = work.tile([P, 1], F32, name="ss", bufs=4)
+            junk = work.tile([P, KV], BF16, name="junk")
+            nc.scalar.activation(junk[:], live["c", n][:], ACT.Square, accum_out=ss[:])
+            live["ss", n] = ss
+
+        def inverse_rms(n):
+            rstd = work.tile([P, 1], F32, name="rstd", bufs=4)
+            nc.scalar.activation(rstd[:], live.pop(("ss", n))[:], ACT.Abs_reciprocal_sqrt, bias=eps[:], scale=1.0 / KV)
             live["rstd", n] = rstd
 
         def make_h(n):
-            rstd = live.pop(("rstd", n))
-            h = work.tile([P, J, KV], BF16, name="h", align_bytes=64)
-            for j in range(J):
-                c = live.pop(("c", n, j))
-                nc.vector.scalar_tensor_tensor(h[:, j, :], c[:], rstd[:, j : j + 1], gain[:], ALU.mult, ALU.mult)
+            h = work.tile([P, KV], BF16, name="h", align_bytes=64)
+            nc.vector.scalar_tensor_tensor(
+                h[:], live.pop(("c", n))[:], live.pop(("rstd", n))[:], gain[:], ALU.mult, ALU.mult
+            )
             live["h", n] = h
 
         def transpose_h(n):
-            words = live.pop(("h", n))[:].rearrange("p j k -> p (j k)").bitcast(F32)
-            ph = psum.tile([P, 2, J, P], F32, name="ph")
-            for j in range(J):
-                for u in range(2):
-                    nc.tensor.transpose(ph[:, u, j, :], words[:, 256 * j + u : 256 * (j + 1) : 2], ident[:])
+            words = live.pop(("h", n))[:].bitcast(F32)
+            ph = psum.tile([P, 2, P], F32, name="ph")
+            for u in range(2):
+                nc.tensor.transpose(ph[:, u, :], words[:, u::2], ident[:])
             live["ph", n] = ph
 
         def copy_h(n):
-            hg = work.tile([P, J * P, 4], BF16, name="hg", align_bytes=64)
+            hg = work.tile([P, P, 4], BF16, name="hg", align_bytes=64)
             nc.scalar.copy(
                 hg[:].rearrange("p r t -> p (r t)").bitcast(F32).rearrange("p (r u) -> p r u", u=2),
-                live.pop(("ph", n))[:].rearrange("p u j r -> p (j r) u"),
+                live.pop(("ph", n))[:].rearrange("p u r -> p r u"),
             )
             live["hg", n] = hg
 
         def quantize_h(n):
-            hc = work.tile([P, J * P], U32, name="hc", align_bytes=64)
-            hcs = work.tile([P, J * P], U8, name="hcs", align_bytes=64)
+            hc = work.tile([P, P], U32, name="hc", align_bytes=64)
+            hcs = work.tile([P, P], U8, name="hcs", align_bytes=64)
             nc.vector.quantize_mx(
                 out=hc[:].bitcast(E4M3X4), scales=hcs[:], in_=live.pop(("hg", n))[:].rearrange("p r t -> p (r t)")
             )
             live["hc", n] = (hc, hcs)
 
-        def matmul_h(n):
+        def matmul_kv(n):
             hc, hcs = live.pop(("hc", n))
-            kv = psum.tile([P, J, N2], F32, name="kv")
-            for j in range(J):
-                cols = slice(j * P, (j + 1) * P)
-                nc.tensor.matmul_mx(
-                    out=kv[:, j, :],
-                    lhsT=hc[:, cols].bitcast(E4M3X4),
-                    lhsT_scale=hcs[:, cols],
-                    rhs=wu[:].bitcast(E2M1X4),
-                    rhs_scale=wus[:],
-                    start=True,
-                    stop=True,
-                )
+            kv = psum.tile([P, N2], F32, name="kv")
+            nc.tensor.matmul_mx(
+                out=kv[:],
+                lhsT=hc[:].bitcast(E4M3X4),
+                lhsT_scale=hcs[:],
+                rhs=wu[:].bitcast(E2M1X4),
+                rhs_scale=wus[:],
+                start=True,
+                stop=True,
+            )
             live["kv", n] = kv
 
-        def kf_tile(n):
-            if ("kf", n) not in live:
-                live["kf", n] = work.tile([P, J, 4, FEAT], F32, name="kf", bufs=4)
-            return live["kf", n]
+        def staging(n):
+            if ("rows", n // J) not in live:
+                live["rows", n // J] = work.tile([P, J, 384], F32, name="rows", bufs=6)
+            return live["rows", n // J]
 
         def copy_r(n):
-            rs = work.tile([P, J, 2, FEAT], F32, name="rs")
-            nc.scalar.copy(rs[:].rearrange("p j d i -> p j (d i)"), live.pop(("r", n))[:])
+            rs = work.tile([P, 2, FEAT], F32, name="rs", bufs=4)
+            nc.scalar.copy(rs[:].rearrange("p d i -> p (d i)"), live.pop(("r", n))[:])
             live["rs", n] = rs
 
         def rope(n):
-            kf = kf_tile(n)
+            out = staging(n)[:, n % J, :].rearrange("p (b i) -> p b i", i=FEAT)
             rs = live.pop(("rs", n))
-            at = slice(n // B * J, (n // B + 1) * J)
-            by_cos = work.tile([P, J, 2, FEAT], F32, name="by_cos")
-            by_sin = work.tile([P, J, 2, FEAT], F32, name="by_sin")
-            shape = [P, J, 2, FEAT]
-            nc.gpsimd.tensor_tensor(by_cos[:], rs[:], cos[:, at].unsqueeze(2).to_broadcast(shape), ALU.mult)
-            nc.gpsimd.tensor_tensor(by_sin[:], rs[:], sin[:, at].unsqueeze(2).to_broadcast(shape), ALU.mult)
-            nc.gpsimd.tensor_tensor(kf[:, :, 1, :], by_cos[:, :, 0, :], by_sin[:, :, 1, :], ALU.subtract)
-            nc.gpsimd.tensor_tensor(kf[:, :, 2, :], by_cos[:, :, 1, :], by_sin[:, :, 0, :], ALU.add)
+            at = n // J // B * J + n % J
+            by_cos = work.tile([P, 2, FEAT], F32, name="by_cos")
+            by_sin = work.tile([P, 2, FEAT], F32, name="by_sin")
+            shape = [P, 2, FEAT]
+            nc.gpsimd.tensor_tensor(by_cos[:], rs[:], cos[:, at].unsqueeze(1).to_broadcast(shape), ALU.mult)
+            nc.gpsimd.tensor_tensor(by_sin[:], rs[:], sin[:, at].unsqueeze(1).to_broadcast(shape), ALU.mult)
+            nc.gpsimd.tensor_tensor(out[:, 1], by_cos[:, 0], by_sin[:, 1], ALU.subtract)
+            nc.gpsimd.tensor_tensor(out[:, 2], by_cos[:, 1], by_sin[:, 0], ALU.add)
 
         def copy_kv(n):
-            kf = kf_tile(n)
-            v = work.tile([P, J, HEADS, FEAT], F32, name="v")
-            kv = live.pop(("kv", n))[:].rearrange("p j (h d i) -> p j h d i", h=HEADS, d=2)
-            nc.scalar.copy(kf[:, :, 0:4:3, :], kv[:, :, :, 0, :])
-            nc.scalar.copy(v[:], kv[:, :, :, 1, :])
-            live["v", n] = v
+            out = staging(n)[:, n % J, :].rearrange("p (b i) -> p b i", i=FEAT)
+            kv = live.pop(("kv", n))[:].rearrange("p (h d i) -> p h d i", h=HEADS, d=2)
+            nc.scalar.copy(out[:, 0:4:3, :], kv[:, :, 0, :])
+            nc.scalar.copy(out[:, 4:6, :], kv[:, :, 1, :])
 
         def store(n):
             at = pair_of[n]
-            kf = live.pop(("kf", n))[:].rearrange("p j b i -> p j (b i)")
-            v = live.pop(("v", n))
-            nc.sync.dma_start(out=kf_hbm[at, :, :, 0:256], in_=kf)
-            nc.sync.dma_start(out=kf_hbm[at, :, :, 256:384], in_=kf[:, :, 64:192])
-            nc.sync.dma_start(out=v_hbm[at], in_=v[:].rearrange("p j h i -> p (j h i)"))
+            rows = live.pop(("rows", n))
+            nc.sync.dma_start(out=kf_hbm[at, :, :, 0:256], in_=rows[:, :, 0:256])
+            nc.sync.dma_start(out=kf_hbm[at, :, :, 256:384], in_=rows[:, :, 64:192])
+            nc.sync.dma_start(out=v_hbm[at], in_=rows[:, :, 256:384])
 
-        def run(stage, n):
-            if 0 <= n < NPAIR:
-                stage(n)
+        def finish(n):
+            copy_kv(n)
+            if n % J == J - 1:
+                store(n // J)
 
-        cast(0)
-        trig_scalar(0)
-        cast(1)
-        for c in range(1, CHUNKS):
-            trig_scalar(c)
-        for c in range(CHUNKS):
-            trig_gpsimd(c)
-        transpose_x(0)
-
-        for s in range(0, NPAIR + 3):
-            run(copy_h, s - 2)
-            run(matmul_x, s - 1)
-            run(norm, s - 1)
-            run(matmul_h, s - 3)
-            run(copy_kv, s - 3)
-            run(scale_x, s)
-            run(make_h, s - 1)
-            run(quantize_x, s)
-            run(quantize_h, s - 2)
-            run(copy_r, s - 1)
-            run(rope, s - 1)
-            run(cast, s + 2)
-            run(transpose_x, s + 1)
-            run(transpose_h, s - 1)
-            run(store, s - 3)
+        stages = (
+            (transpose_x, 1),
+            (copy_r, -3),
+            (finish, -7),
+            (copy_h, -5),
+            (sum_squares, -3),
+            (matmul_c, -2),
+            (make_h, -4),
+            (cast, 4),
+            (inverse_rms, -3),
+            (quantize_x, 0),
+            (quantize_h, -5),
+            (matmul_kv, -6),
+            (matmul_r, -2),
+            (rope, -3),
+            (scale_x, 1),
+            (transpose_h, -4),
+        )
+        for step in range(-4, NTILE + 7):
+            for stage, ahead in stages:
+                if 0 <= step + ahead < NTILE:
+                    stage(step + ahead)
+            if step == -3:
+                for c in range(CHUNKS):
+                    trig_scalar(c)
+                for c in range(CHUNKS):
+                    trig_gpsimd(c)

@@ -31,7 +31,8 @@ PER_B = S // PAIR
 G1 = D // 512
 CHUNKS = 4
 NTILE = NPAIR * J
-ON_VECTOR = 192
+ON_VECTOR = 256
+ON_VECTOR_FIRST = 640
 
 
 def tile_multiheadlatentattention_pb_t_w4_kernel(
@@ -68,7 +69,7 @@ def tile_multiheadlatentattention_pb_t_w4_kernel(
         frac = keep.tile([P, PER_B * J, FEAT], F32, name="frac")
         half = keep.tile([P, PER_B * J, FEAT], F32, name="half")
         square = keep.tile([P, PER_B * J, FEAT], F32, name="square")
-        sin = keep.tile([P, PER_B * J, FEAT], F32, name="sin")
+        sin = keep.tile([P, PER_B * J, 2, FEAT], F32, name="sin")
         cos = keep.tile([P, PER_B * J, FEAT], F32, name="cos")
 
         nc.vector.memset(one[:], 1.0)
@@ -127,16 +128,14 @@ def tile_multiheadlatentattention_pb_t_w4_kernel(
                 theta[:].unsqueeze(1).to_broadcast([P, rows, FEAT]),
                 ALU.mult,
             )
+
+        def trig(c):
+            sl = slice(c * rows, (c + 1) * rows)
             nc.vector.tensor_copy(whole[:, sl], turns[:, sl])
             nc.vector.tensor_tensor(frac[:, sl], turns[:, sl], whole[:, sl], ALU.subtract)
-
-        def trig_scalar(c):
-            sl = slice(c * rows, (c + 1) * rows)
             nc.scalar.activation(half[:, sl], frac[:, sl], ACT.Sin, scale=math.pi)
-            nc.scalar.activation(sin[:, sl], frac[:, sl], ACT.Sin, scale=2.0 * math.pi)
-
-        def trig_gpsimd(c):
-            sl = slice(c * rows, (c + 1) * rows)
+            nc.scalar.activation(sin[:, sl, 1], frac[:, sl], ACT.Sin, scale=2.0 * math.pi)
+            nc.gpsimd.tensor_scalar(sin[:, sl, 0], sin[:, sl, 1], -1.0, 0.0, ALU.mult, ALU.add)
             nc.gpsimd.tensor_tensor(square[:, sl], half[:, sl], half[:, sl], ALU.mult)
             nc.gpsimd.tensor_scalar(cos[:, sl], square[:, sl], -2.0, 1.0, ALU.mult, ALU.add)
 
@@ -145,8 +144,8 @@ def tile_multiheadlatentattention_pb_t_w4_kernel(
         def cast(n):
             xw = work.tile([P, D], BF16, name="xw", bufs=7, align_bytes=64)
             codes = xb[:, n // J, n % J * D : (n % J + 1) * D]
-            cut = D - ON_VECTOR
-            nc.scalar.copy(xw[:, :cut], codes[:, :cut].bitcast(FP8))
+            cut = D - (ON_VECTOR_FIRST if n < 4 else ON_VECTOR)
+            nc.scalar.activation(xw[:, :cut], codes[:, :cut].bitcast(FP8), ACT.Copy)
             nc.vector.tensor_copy(xw[:, cut:], codes[:, cut:].bitcast(FP8))
             live["xw", n] = xw
 
@@ -276,9 +275,8 @@ def tile_multiheadlatentattention_pb_t_w4_kernel(
             by_sin = work.tile([P, 2, FEAT], F32, name="by_sin")
             shape = [P, 2, FEAT]
             nc.gpsimd.tensor_tensor(by_cos[:], rs[:], cos[:, at].unsqueeze(1).to_broadcast(shape), ALU.mult)
-            nc.gpsimd.tensor_tensor(by_sin[:], rs[:], sin[:, at].unsqueeze(1).to_broadcast(shape), ALU.mult)
-            nc.gpsimd.tensor_tensor(out[:, 1], by_cos[:, 0], by_sin[:, 1], ALU.subtract)
-            nc.gpsimd.tensor_tensor(out[:, 2], by_cos[:, 1], by_sin[:, 0], ALU.add)
+            nc.gpsimd.tensor_tensor(by_sin[:], rs[:, ::-1, :], sin[:, at], ALU.mult)
+            nc.gpsimd.tensor_tensor(out[:, 1:3], by_cos[:], by_sin[:], ALU.add)
 
         def copy_kv(n):
             out = staging(n)[:, n % J, :].rearrange("p (b i) -> p b i", i=FEAT)
@@ -320,8 +318,5 @@ def tile_multiheadlatentattention_pb_t_w4_kernel(
             for stage, ahead in stages:
                 if 0 <= step + ahead < NTILE:
                     stage(step + ahead)
-            if step == -3:
-                for c in range(CHUNKS):
-                    trig_scalar(c)
-                for c in range(CHUNKS):
-                    trig_gpsimd(c)
+            if 0 <= step + 2 < CHUNKS:
+                trig(step + 2)

@@ -30,8 +30,6 @@ NPAIR = TOK // PAIR
 PER_B = S // PAIR
 G1 = D // 512
 CHUNKS = 4
-NTILE = NPAIR * J
-ON_VECTOR = 256
 ON_VECTOR_FIRST = 640
 
 
@@ -144,9 +142,10 @@ def tile_multiheadlatentattention_pb_t_w4_kernel(
         def cast(n):
             xw = work.tile([P, D], BF16, name="xw", bufs=7, align_bytes=64)
             codes = xb[:, n // J, n % J * D : (n % J + 1) * D]
-            cut = D - (ON_VECTOR_FIRST if n < 4 else ON_VECTOR)
-            nc.scalar.activation(xw[:, :cut], codes[:, :cut].bitcast(FP8), ACT.Copy)
-            nc.vector.tensor_copy(xw[:, cut:], codes[:, cut:].bitcast(FP8))
+            cut = D - ON_VECTOR_FIRST if n < 2 * J else D
+            nc.scalar.copy(xw[:, :cut], codes[:, :cut].bitcast(FP8))
+            if cut < D:
+                nc.vector.tensor_copy(xw[:, cut:], codes[:, cut:].bitcast(FP8))
             live["xw", n] = xw
 
         def transpose_x(n):
@@ -158,29 +157,29 @@ def tile_multiheadlatentattention_pb_t_w4_kernel(
             live["px", n] = px
 
         def scale_x(n):
-            xg = work.tile([P, D // 2, 2], BF16, name="xg", align_bytes=64)
+            if n % J == 0:
+                live["xg", n // J] = work.tile([P, J, D // 2, 2], BF16, name="xg", align_bytes=64)
             nc.vector.tensor_tensor(
-                xg[:].rearrange("p (g r u) e -> p g r u e", g=G1, u=2),
+                live["xg", n // J][:, n % J].rearrange("p (g r u) e -> p g r u e", g=G1, u=2),
                 live.pop(("px", n))[:].rearrange("p u g r -> p (u g r)").bitcast(BF16).rearrange(
                     "p (u g r e) -> p g r u e", u=2, g=G1, e=2
                 ),
                 xs[:].rearrange("p g (u e) -> p g u e", u=2).unsqueeze(2).to_broadcast([P, G1, P, 2, 2]),
                 ALU.mult,
             )
-            live["xg", n] = xg
 
-        def quantize_x(n):
-            xc = work.tile([P, G1 * P], U32, name="xc", bufs=5, align_bytes=64)
-            xcs = work.tile([P, G1 * P], U8, name="xcs", bufs=5, align_bytes=64)
+        def quantize_x(k):
+            xc = work.tile([P, J * G1 * P], U32, name="xc", align_bytes=64)
+            xcs = work.tile([P, J * G1 * P], U8, name="xcs", align_bytes=64)
             nc.vector.quantize_mx(
-                out=xc[:].bitcast(E4M3X4), scales=xcs[:], in_=live.pop(("xg", n))[:].rearrange("p w e -> p (w e)")
+                out=xc[:].bitcast(E4M3X4), scales=xcs[:], in_=live.pop(("xg", k))[:].rearrange("p j w e -> p (j w e)")
             )
-            live["xc", n] = (xc, xcs)
+            live["xc", k] = (xc, xcs)
 
         def matmul_x(out, n, lo, hi):
-            xc, xcs = live["xc", n]
+            xc, xcs = live["xc", n // J]
             for g in range(G1):
-                cols = slice(g * P, (g + 1) * P)
+                cols = slice((n % J * G1 + g) * P, (n % J * G1 + g + 1) * P)
                 nc.tensor.matmul_mx(
                     out=out,
                     lhsT=xc[:, cols].bitcast(E4M3X4),
@@ -196,11 +195,12 @@ def tile_multiheadlatentattention_pb_t_w4_kernel(
             matmul_x(c[:], n, 0, KV)
             live["c", n] = c
 
-        def matmul_r(n):
-            r = psum.tile([P, ROPE], F32, name="r")
-            matmul_x(r[:], n, KV, N1)
-            live["r", n] = r
-            live.pop(("xc", n))
+        def matmul_r(k):
+            r = psum.tile([P, J, ROPE], F32, name="r")
+            for j in range(J):
+                matmul_x(r[:, j, :], J * k + j, KV, N1)
+            live["r", k] = r
+            live.pop(("xc", k))
 
         def sum_squares(n):
             ss = work.tile([P, 1], F32, name="ss", bufs=4)
@@ -214,109 +214,120 @@ def tile_multiheadlatentattention_pb_t_w4_kernel(
             live["rstd", n] = rstd
 
         def make_h(n):
-            h = work.tile([P, KV], BF16, name="h", align_bytes=64)
+            h = work.tile([P, KV], BF16, name="h", bufs=4, align_bytes=64)
             nc.vector.scalar_tensor_tensor(
                 h[:], live.pop(("c", n))[:], live.pop(("rstd", n))[:], gain[:], ALU.mult, ALU.mult
             )
             live["h", n] = h
 
         def transpose_h(n):
+            if n % J == 0:
+                live["ph", n // J] = psum.tile([P, 2, J, P], F32, name="ph")
             words = live.pop(("h", n))[:].bitcast(F32)
-            ph = psum.tile([P, 2, P], F32, name="ph")
             for u in range(2):
-                nc.tensor.transpose(ph[:, u, :], words[:, u::2], ident[:])
-            live["ph", n] = ph
+                nc.tensor.transpose(live["ph", n // J][:, u, n % J, :], words[:, u::2], ident[:])
 
-        def copy_h(n):
-            hg = work.tile([P, P, 4], BF16, name="hg", align_bytes=64)
+        def copy_h(k):
+            hg = work.tile([P, J * P, 4], BF16, name="hg", align_bytes=64)
             nc.scalar.copy(
                 hg[:].rearrange("p r t -> p (r t)").bitcast(F32).rearrange("p (r u) -> p r u", u=2),
-                live.pop(("ph", n))[:].rearrange("p u r -> p r u"),
+                live.pop(("ph", k))[:].rearrange("p u j r -> p (j r) u"),
             )
-            live["hg", n] = hg
+            live["hg", k] = hg
 
-        def quantize_h(n):
-            hc = work.tile([P, P], U32, name="hc", align_bytes=64)
-            hcs = work.tile([P, P], U8, name="hcs", align_bytes=64)
+        def quantize_h(k):
+            hc = work.tile([P, J * P], U32, name="hc", align_bytes=64)
+            hcs = work.tile([P, J * P], U8, name="hcs", align_bytes=64)
             nc.vector.quantize_mx(
-                out=hc[:].bitcast(E4M3X4), scales=hcs[:], in_=live.pop(("hg", n))[:].rearrange("p r t -> p (r t)")
+                out=hc[:].bitcast(E4M3X4), scales=hcs[:], in_=live.pop(("hg", k))[:].rearrange("p r t -> p (r t)")
             )
-            live["hc", n] = (hc, hcs)
+            live["hc", k] = (hc, hcs)
 
-        def matmul_kv(n):
-            hc, hcs = live.pop(("hc", n))
-            kv = psum.tile([P, N2], F32, name="kv")
-            nc.tensor.matmul_mx(
-                out=kv[:],
-                lhsT=hc[:].bitcast(E4M3X4),
-                lhsT_scale=hcs[:],
-                rhs=wu[:].bitcast(E2M1X4),
-                rhs_scale=wus[:],
-                start=True,
-                stop=True,
+        def matmul_kv(k):
+            hc, hcs = live.pop(("hc", k))
+            kv = psum.tile([P, J, N2], F32, name="kv")
+            for j in range(J):
+                cols = slice(j * P, (j + 1) * P)
+                nc.tensor.matmul_mx(
+                    out=kv[:, j, :],
+                    lhsT=hc[:, cols].bitcast(E4M3X4),
+                    lhsT_scale=hcs[:, cols],
+                    rhs=wu[:].bitcast(E2M1X4),
+                    rhs_scale=wus[:],
+                    start=True,
+                    stop=True,
+                )
+            live["kv", k] = kv
+
+        def copy_r(k):
+            rs = work.tile([P, J, 2, FEAT], F32, name="rs")
+            nc.scalar.copy(rs[:].rearrange("p j d i -> p j (d i)"), live.pop(("r", k))[:])
+            live["rs", k] = rs
+
+        def rope(k):
+            rows = work.tile([P, J, 6, FEAT], F32, name="rows", bufs=5)
+            live["rows", k] = rows
+            rs = live.pop(("rs", k))
+            at = slice(k // B * J, (k // B + 1) * J)
+            by_cos = work.tile([P, J, 2, FEAT], F32, name="by_cos")
+            by_sin = work.tile([P, J, 2, FEAT], F32, name="by_sin")
+            nc.gpsimd.tensor_tensor(
+                by_cos[:], rs[:], cos[:, at].unsqueeze(2).to_broadcast([P, J, 2, FEAT]), ALU.mult
             )
-            live["kv", n] = kv
+            nc.gpsimd.tensor_tensor(by_sin[:], rs[:, :, ::-1, :], sin[:, at], ALU.mult)
+            nc.gpsimd.tensor_tensor(rows[:, :, 1:3, :], by_cos[:], by_sin[:], ALU.add)
 
-        def staging(n):
-            if ("rows", n // J) not in live:
-                live["rows", n // J] = work.tile([P, J, 384], F32, name="rows", bufs=6)
-            return live["rows", n // J]
+        def copy_k(k):
+            kv = live["kv", k][:].rearrange("p j (h d i) -> p j h d i", h=HEADS, d=2)
+            nc.scalar.copy(live["rows", k][:, :, 0:4:3, :], kv[:, :, :, 0, :])
 
-        def copy_r(n):
-            rs = work.tile([P, 2, FEAT], F32, name="rs", bufs=4)
-            nc.scalar.copy(rs[:].rearrange("p d i -> p (d i)"), live.pop(("r", n))[:])
-            live["rs", n] = rs
-
-        def rope(n):
-            out = staging(n)[:, n % J, :].rearrange("p (b i) -> p b i", i=FEAT)
-            rs = live.pop(("rs", n))
-            at = n // J // B * J + n % J
-            by_cos = work.tile([P, 2, FEAT], F32, name="by_cos")
-            by_sin = work.tile([P, 2, FEAT], F32, name="by_sin")
-            shape = [P, 2, FEAT]
-            nc.gpsimd.tensor_tensor(by_cos[:], rs[:], cos[:, at].unsqueeze(1).to_broadcast(shape), ALU.mult)
-            nc.gpsimd.tensor_tensor(by_sin[:], rs[:, ::-1, :], sin[:, at], ALU.mult)
-            nc.gpsimd.tensor_tensor(out[:, 1:3], by_cos[:], by_sin[:], ALU.add)
-
-        def copy_kv(n):
-            out = staging(n)[:, n % J, :].rearrange("p (b i) -> p b i", i=FEAT)
-            kv = live.pop(("kv", n))[:].rearrange("p (h d i) -> p h d i", h=HEADS, d=2)
-            nc.scalar.copy(out[:, 0:4:3, :], kv[:, :, 0, :])
-            nc.scalar.copy(out[:, 4:6, :], kv[:, :, 1, :])
-
-        def store(n):
-            at = pair_of[n]
-            rows = live.pop(("rows", n))
+        def copy_v(k):
+            kv = live.pop(("kv", k))[:].rearrange("p j (h d i) -> p j h d i", h=HEADS, d=2)
+            rows = live.pop(("rows", k))
+            nc.scalar.copy(rows[:, :, 4:6, :], kv[:, :, :, 1, :])
+            rows = rows[:].rearrange("p j b i -> p j (b i)")
+            at = pair_of[k]
             nc.sync.dma_start(out=kf_hbm[at, :, :, 0:256], in_=rows[:, :, 0:256])
             nc.sync.dma_start(out=kf_hbm[at, :, :, 256:384], in_=rows[:, :, 64:192])
             nc.sync.dma_start(out=v_hbm[at], in_=rows[:, :, 256:384])
 
-        def finish(n):
-            copy_kv(n)
-            if n % J == J - 1:
-                store(n // J)
+        def first(stage):
+            return lambda k: stage(J * k)
+
+        def second(stage):
+            return lambda k: stage(J * k + 1)
 
         stages = (
-            (transpose_x, 1),
-            (copy_r, -3),
-            (finish, -7),
-            (copy_h, -5),
-            (sum_squares, -3),
-            (matmul_c, -2),
-            (make_h, -4),
-            (cast, 4),
-            (inverse_rms, -3),
+            (copy_r, -2),
+            (first(matmul_c), -1),
+            (matmul_kv, -3),
+            (first(scale_x), 0),
+            (first(cast), 2),
+            (first(sum_squares), -1),
+            (copy_k, -3),
+            (first(inverse_rms), -1),
+            (copy_v, -3),
+            (second(make_h), -2),
+            (first(transpose_x), 1),
+            (second(transpose_h), -2),
+            (second(matmul_c), -1),
+            (matmul_r, -1),
+            (second(scale_x), 0),
+            (first(make_h), -1),
+            (copy_h, -2),
+            (second(sum_squares), -1),
+            (second(cast), 2),
+            (second(inverse_rms), -1),
+            (second(transpose_x), 1),
+            (first(transpose_h), -1),
             (quantize_x, 0),
-            (quantize_h, -5),
-            (matmul_kv, -6),
-            (matmul_r, -2),
-            (rope, -3),
-            (scale_x, 1),
-            (transpose_h, -4),
+            (quantize_h, -2),
+            (rope, -2),
         )
-        for step in range(-4, NTILE + 7):
+        chunks_in = {-2: (0,), -1: (1,), 0: (2, 3)}
+        for step in range(-2, NPAIR + 3):
             for stage, ahead in stages:
-                if 0 <= step + ahead < NTILE:
+                if 0 <= step + ahead < NPAIR:
                     stage(step + ahead)
-            if 0 <= step + 2 < CHUNKS:
-                trig(step + 2)
+            for c in chunks_in.get(step, ()):
+                trig(c)

@@ -30,7 +30,9 @@ NPAIR = TOK // PAIR
 PER_B = S // PAIR
 G1 = D // 512
 CHUNKS = 4
-ON_VECTOR_FIRST = 640
+ROWS = PER_B * J // CHUNKS
+STEPS = CHUNKS - 1
+ANGLED = STEPS + ROWS
 
 
 def tile_multiheadlatentattention_pb_t_w4_kernel(
@@ -60,15 +62,15 @@ def tile_multiheadlatentattention_pb_t_w4_kernel(
         eps = keep.tile([P, 1], F32, name="eps")
         one = keep.tile([P, 1], F32, name="one")
         dummy = keep.tile([P, 1], F32, name="dummy")
-        pos = keep.tile([P, PER_B * J], F32, name="pos")
+        pos = keep.tile([P, ANGLED], F32, name="pos")
         theta = keep.tile([P, FEAT], F32, name="theta")
-        turns = keep.tile([P, PER_B * J, FEAT], F32, name="turns")
-        whole = keep.tile([P, PER_B * J, FEAT], I32, name="whole")
-        frac = keep.tile([P, PER_B * J, FEAT], F32, name="frac")
-        half = keep.tile([P, PER_B * J, FEAT], F32, name="half")
-        square = keep.tile([P, PER_B * J, FEAT], F32, name="square")
-        sin = keep.tile([P, PER_B * J, 2, FEAT], F32, name="sin")
-        cos = keep.tile([P, PER_B * J, FEAT], F32, name="cos")
+        turns = keep.tile([P, ANGLED, FEAT], F32, name="turns")
+        whole = keep.tile([P, ANGLED, FEAT], I32, name="whole")
+        frac = keep.tile([P, ANGLED, FEAT], F32, name="frac")
+        half = keep.tile([P, ANGLED, FEAT], F32, name="half")
+        square = keep.tile([P, ANGLED, FEAT], F32, name="square")
+        sin = keep.tile([P, STEPS + PER_B * J, FEAT], F32, name="sin")
+        cos = keep.tile([P, STEPS + PER_B * J, FEAT], F32, name="cos")
 
         nc.vector.memset(one[:], 1.0)
         nc.vector.memset(wds[:].rearrange("p g n -> p (g n)").bitcast(I32), 0)
@@ -78,12 +80,9 @@ def tile_multiheadlatentattention_pb_t_w4_kernel(
         def load_x(n):
             nc.sync.dma_start(out=xb[:, n, :], in_=xb_hbm[pair_of[n]])
 
-        for j in range(J):
-            cols = slice(j * D, (j + 1) * D)
-            nc.sync.dma_start(out=xb[:, 0, cols], in_=xb_hbm[pair_of[0], :, cols])
-        nc.sync.dma_start(
-            out=xs[:], in_=x_scale.rearrange("a b (g p t) -> p (a b g) t", p=P, t=4)
-        )
+        nc.sync.dma_start(out=xb[:, 0, :D], in_=xb_hbm[pair_of[0], :, :D])
+        nc.sync.dma_start(out=xs[:], in_=x_scale.rearrange("a b (g p t) -> p (a b g) t", p=P, t=4))
+        nc.sync.dma_start(out=xb[:, 0, D:], in_=xb_hbm[pair_of[0], :, D:])
         load_x(1)
         nc.sync.dma_start(
             out=wd[:].bitcast(I32),
@@ -105,47 +104,61 @@ def tile_multiheadlatentattention_pb_t_w4_kernel(
         for n in range(3, NPAIR):
             load_x(n)
 
-        make_identity(nc, ident[:])
         nc.gpsimd.iota(
-            pos[:], [[PAIR, PER_B], [1, J]], base=0, channel_multiplier=J, allow_small_or_imprecise_dtypes=True
+            pos[:, :STEPS],
+            [[PAIR * PER_B // CHUNKS, STEPS]],
+            base=PAIR * PER_B // CHUNKS,
+            channel_multiplier=0,
+            allow_small_or_imprecise_dtypes=True,
         )
-        nc.vector.tensor_scalar(theta[:, 0:1], one[:], 1.0 / (2.0 * math.pi), None, ALU.mult)
-        nc.vector.tensor_scalar(eps[:], one[:], -1.0, EPS, ALU.add, ALU.add)
-        width = 1
-        while width < FEAT:
-            nc.vector.tensor_scalar(
-                theta[:, width : 2 * width], theta[:, 0:width], THETA ** (-width / FEAT), None, ALU.mult
-            )
-            width *= 2
-        rows = PER_B * J // CHUNKS
-        for c in range(CHUNKS):
-            sl = slice(c * rows, (c + 1) * rows)
-            nc.gpsimd.tensor_tensor(
-                turns[:, sl],
-                pos[:, sl].unsqueeze(2).to_broadcast([P, rows, FEAT]),
-                theta[:].unsqueeze(1).to_broadcast([P, rows, FEAT]),
-                ALU.mult,
-            )
+        nc.gpsimd.iota(
+            pos[:, STEPS:],
+            [[PAIR, ROWS // J], [1, J]],
+            base=0,
+            channel_multiplier=J,
+            allow_small_or_imprecise_dtypes=True,
+        )
+        make_identity(nc, ident[:])
 
-        def trig(c):
-            sl = slice(c * rows, (c + 1) * rows)
-            nc.vector.tensor_copy(whole[:, sl], turns[:, sl])
-            nc.vector.tensor_tensor(frac[:, sl], turns[:, sl], whole[:, sl], ALU.subtract)
-            nc.scalar.activation(half[:, sl], frac[:, sl], ACT.Sin, scale=math.pi)
-            nc.scalar.activation(sin[:, sl, 1], frac[:, sl], ACT.Sin, scale=2.0 * math.pi)
-            nc.gpsimd.tensor_scalar(sin[:, sl, 0], sin[:, sl, 1], -1.0, 0.0, ALU.mult, ALU.add)
-            nc.gpsimd.tensor_tensor(square[:, sl], half[:, sl], half[:, sl], ALU.mult)
-            nc.gpsimd.tensor_scalar(cos[:, sl], square[:, sl], -2.0, 1.0, ALU.mult, ALU.add)
+        for i in range(8):
+            nc.vector.tensor_scalar(
+                theta[:, i : i + 1], one[:], THETA ** (-i / FEAT) / (2.0 * math.pi), None, ALU.mult
+            )
+        nc.vector.tensor_scalar(eps[:], one[:], -1.0, EPS, ALU.add, ALU.add)
+        for i in range(8, FEAT, 8):
+            nc.vector.tensor_scalar(theta[:, i : i + 8], theta[:, 0:8], THETA ** (-i / FEAT), None, ALU.mult)
+        shape = [P, ANGLED, FEAT]
+        nc.vector.tensor_tensor(
+            turns[:], pos[:].unsqueeze(2).to_broadcast(shape), theta[:].unsqueeze(1).to_broadcast(shape), ALU.mult
+        )
+        nc.vector.tensor_copy(whole[:], turns[:])
+        nc.vector.tensor_tensor(frac[:], turns[:], whole[:], ALU.subtract)
+
+        def first_tables():
+            nc.scalar.activation(half[:], frac[:], ACT.Sin, scale=math.pi)
+            nc.scalar.activation(sin[:, :ANGLED], frac[:], ACT.Sin, scale=2.0 * math.pi)
+            nc.gpsimd.tensor_tensor(square[:], half[:], half[:], ALU.mult)
+            nc.gpsimd.tensor_scalar(cos[:, :ANGLED], square[:], -2.0, 1.0, ALU.mult, ALU.add)
+
+        def turn_tables(c):
+            base = slice(STEPS, ANGLED)
+            new = slice(STEPS + c * ROWS, STEPS + (c + 1) * ROWS)
+            shape = [P, ROWS, FEAT]
+            cos_by = cos[:, c - 1].unsqueeze(1).to_broadcast(shape)
+            sin_by = sin[:, c - 1].unsqueeze(1).to_broadcast(shape)
+            for table, a, b, op in ((cos, cos, sin, ALU.subtract), (sin, sin, cos, ALU.add)):
+                left = work.tile(shape, F32, name="left", bufs=2)
+                right = work.tile(shape, F32, name="right", bufs=2)
+                nc.gpsimd.tensor_tensor(left[:], a[:, base], cos_by, ALU.mult)
+                nc.gpsimd.tensor_tensor(right[:], b[:, base], sin_by, ALU.mult)
+                nc.gpsimd.tensor_tensor(table[:, new], left[:], right[:], op)
 
         live = {}
 
         def cast(n):
             xw = work.tile([P, D], BF16, name="xw", bufs=7, align_bytes=64)
             codes = xb[:, n // J, n % J * D : (n % J + 1) * D]
-            cut = D - ON_VECTOR_FIRST if n < 2 * J else D
-            nc.scalar.copy(xw[:, :cut], codes[:, :cut].bitcast(FP8))
-            if cut < D:
-                nc.vector.tensor_copy(xw[:, cut:], codes[:, cut:].bitcast(FP8))
+            nc.scalar.copy(xw[:], codes.bitcast(FP8))
             live["xw", n] = xw
 
         def transpose_x(n):
@@ -268,14 +281,14 @@ def tile_multiheadlatentattention_pb_t_w4_kernel(
             rows = work.tile([P, J, 6, FEAT], F32, name="rows", bufs=5)
             live["rows", k] = rows
             rs = live.pop(("rs", k))
-            at = slice(k // B * J, (k // B + 1) * J)
+            at = slice(STEPS + k // B * J, STEPS + (k // B + 1) * J)
+            shape = [P, J, 2, FEAT]
             by_cos = work.tile([P, J, 2, FEAT], F32, name="by_cos")
             by_sin = work.tile([P, J, 2, FEAT], F32, name="by_sin")
-            nc.gpsimd.tensor_tensor(
-                by_cos[:], rs[:], cos[:, at].unsqueeze(2).to_broadcast([P, J, 2, FEAT]), ALU.mult
-            )
-            nc.gpsimd.tensor_tensor(by_sin[:], rs[:, :, ::-1, :], sin[:, at], ALU.mult)
-            nc.gpsimd.tensor_tensor(rows[:, :, 1:3, :], by_cos[:], by_sin[:], ALU.add)
+            nc.gpsimd.tensor_tensor(by_cos[:], rs[:], cos[:, at].unsqueeze(2).to_broadcast(shape), ALU.mult)
+            nc.gpsimd.tensor_tensor(by_sin[:], rs[:], sin[:, at].unsqueeze(2).to_broadcast(shape), ALU.mult)
+            nc.gpsimd.tensor_tensor(rows[:, :, 1, :], by_cos[:, :, 0, :], by_sin[:, :, 1, :], ALU.subtract)
+            nc.gpsimd.tensor_tensor(rows[:, :, 2, :], by_cos[:, :, 1, :], by_sin[:, :, 0, :], ALU.add)
 
         def copy_k(k):
             kv = live["kv", k][:].rearrange("p j (h d i) -> p j h d i", h=HEADS, d=2)
@@ -324,10 +337,46 @@ def tile_multiheadlatentattention_pb_t_w4_kernel(
             (quantize_h, -2),
             (rope, -2),
         )
-        chunks_in = {-2: (0,), -1: (1,), 0: (2, 3)}
-        for step in range(-2, NPAIR + 3):
+        drain = (
+            (copy_r, -1),
+            (second(make_h), -1),
+            (first(matmul_c), 0),
+            (second(matmul_c), 0),
+            (second(transpose_h), -1),
+            (matmul_kv, -2),
+            (matmul_r, 0),
+            (first(sum_squares), 0),
+            (second(sum_squares), 0),
+            (first(inverse_rms), 0),
+            (second(inverse_rms), 0),
+            (copy_h, -1),
+            (copy_k, -2),
+            (copy_v, -2),
+            (first(make_h), 0),
+            (first(transpose_h), 0),
+            (second(make_h), 0),
+            (second(transpose_h), 0),
+            (quantize_h, -1),
+            (rope, -1),
+            (copy_r, 0),
+            (copy_h, 0),
+            (matmul_kv, -1),
+            (quantize_h, 0),
+            (rope, 0),
+            (copy_k, -1),
+            (copy_v, -1),
+            (matmul_kv, 0),
+            (copy_k, 0),
+            (copy_v, 0),
+        )
+        for step in range(-2, NPAIR):
             for stage, ahead in stages:
                 if 0 <= step + ahead < NPAIR:
                     stage(step + ahead)
-            for c in chunks_in.get(step, ()):
-                trig(c)
+            if step == -1:
+                first_tables()
+            c = (step + 2) // 4
+            if (step + 2) % 4 == 0 and 0 < c < CHUNKS:
+                turn_tables(c)
+        for stage, ahead in drain:
+            stage(NPAIR - 1 + ahead)

import math
from contextlib import ExitStack

import concourse.mybir as mybir
from concourse.masks import make_identity

F32 = mybir.dt.float32
BF16 = mybir.dt.bfloat16
I32 = mybir.dt.int32
U32 = mybir.dt.uint32
U8 = mybir.dt.uint8
FP8 = mybir.dt.float8_e4m3fn
E4M3X4 = mybir.dt.float8_e4m3fn_x4
E2M1X4 = mybir.dt.float4_e2m1fn_x4
ALU = mybir.AluOpType
ACT = mybir.ActivationFunctionType

B, S, D, KV, ROPE, HEADS, FEAT = 2, 2048, 1024, 512, 128, 2, 64
TOK = B * S
N1 = KV + ROPE
N2 = HEADS * 2 * FEAT
P = 128
EPS = 1e-6
THETA = 10000.0
FLOPS = 2 * TOK * D * N1 + 2 * TOK * KV * N2

J = 2
PAIR = P * J
NPAIR = TOK // PAIR
PER_B = S // PAIR
G1 = D // 512
CHUNKS = 4
ROWS = PER_B * J // CHUNKS
STEPS = CHUNKS - 1
ANGLED = STEPS + ROWS


def tile_multiheadlatentattention_pb_t_w4_kernel(
    tc, x_bytes, x_scale, w_dkv_words, w_dkv_scales, kv_a_norm, w_ukv_words, w_ukv_scales, out_0, out_1
):
    nc = tc.nc
    pair_of = [(n % B) * PER_B + n // B for n in range(NPAIR)]

    xb_hbm = x_bytes.rearrange("b s k -> (b s) k").rearrange("(n p j) k -> n p (j k)", p=P, j=J)
    kf_hbm = out_0.rearrange("b s h c -> (b s) (h c)").rearrange("(n p j) c -> n p j c", p=P, j=J)
    v_hbm = out_1.rearrange("b s h c -> (b s) (h c)").rearrange("(n p j) c -> n p j c", p=P, j=J)

    with ExitStack() as ctx:
        keep = ctx.enter_context(tc.tile_pool(name="keep", bufs=1))
        work = ctx.enter_context(tc.tile_pool(name="work", bufs=3))
        psum = ctx.enter_context(tc.psum_pool(name="psum", bufs=1))
        ctx.enter_context(tc.manual_schedule())

        xb = keep.tile([P, NPAIR, J * D], U8, name="xb", align_bytes=64)
        xs = keep.tile([P, G1, 4], F32, name="xs", align_bytes=64)
        wd = keep.tile([P, G1, 2 * N1], U8, name="wd", align_bytes=64)
        wds = keep.tile([P, G1, N1], U8, name="wds", align_bytes=64)
        wu = keep.tile([P, 2 * N2], U8, name="wu", align_bytes=64)
        wus = keep.tile([P, N2], U8, name="wus", align_bytes=64)
        gain = keep.tile([P, KV], BF16, name="gain", align_bytes=64)
        ident = keep.tile([P, P], F32, name="ident", align_bytes=64)
        eps = keep.tile([P, 1], F32, name="eps")
        one = keep.tile([P, 1], F32, name="one")
        dummy = keep.tile([P, 1], F32, name="dummy")
        pos = keep.tile([P, ANGLED], F32, name="pos")
        theta = keep.tile([P, FEAT], F32, name="theta")
        turns = keep.tile([P, ANGLED, FEAT], F32, name="turns")
        whole = keep.tile([P, ANGLED, FEAT], I32, name="whole")
        frac = keep.tile([P, ANGLED, FEAT], F32, name="frac")
        half = keep.tile([P, ANGLED, FEAT], F32, name="half")
        square = keep.tile([P, ANGLED, FEAT], F32, name="square")
        sin = keep.tile([P, STEPS + PER_B * J, FEAT], F32, name="sin")
        cos = keep.tile([P, STEPS + PER_B * J, FEAT], F32, name="cos")

        nc.vector.memset(one[:], 1.0)
        nc.vector.memset(wds[:].rearrange("p g n -> p (g n)").bitcast(I32), 0)
        nc.vector.memset(wus[:].bitcast(I32), 0)
        nc.scalar.activation(dummy[:], one[:], ACT.Sin)

        def load_x(n):
            nc.sync.dma_start(out=xb[:, n, :], in_=xb_hbm[pair_of[n]])

        nc.sync.dma_start(out=xb[:, 0, :D], in_=xb_hbm[pair_of[0], :, :D])
        nc.sync.dma_start(out=xs[:], in_=x_scale.rearrange("a b (g p t) -> p (a b g) t", p=P, t=4))
        nc.sync.dma_start(out=xb[:, 0, D:], in_=xb_hbm[pair_of[0], :, D:])
        load_x(1)
        nc.sync.dma_start(
            out=wd[:].bitcast(I32),
            in_=w_dkv_words.rearrange("g p n -> p g n").bitcast(I32),
        )
        for q in range(4):
            nc.sync.dma_start(
                out=wds[32 * q : 32 * q + 4].bitcast(I32),
                in_=w_dkv_scales[:, 4 * q : 4 * q + 4, :].rearrange("g q n -> q g n").bitcast(I32),
            )
        for q in range(4):
            nc.sync.dma_start(
                out=wus[32 * q : 32 * q + 4].bitcast(I32),
                in_=w_ukv_scales[0, 4 * q : 4 * q + 4, :].bitcast(I32),
            )
        nc.sync.dma_start(out=gain[:], in_=kv_a_norm.partition_broadcast(P))
        load_x(2)
        nc.sync.dma_start(out=wu[:].bitcast(I32), in_=w_ukv_words[0].bitcast(I32))
        for n in range(3, NPAIR):
            load_x(n)

        nc.gpsimd.iota(
            pos[:, :STEPS],
            [[PAIR * PER_B // CHUNKS, STEPS]],
            base=PAIR * PER_B // CHUNKS,
            channel_multiplier=0,
            allow_small_or_imprecise_dtypes=True,
        )
        nc.gpsimd.iota(
            pos[:, STEPS:],
            [[PAIR, ROWS // J], [1, J]],
            base=0,
            channel_multiplier=J,
            allow_small_or_imprecise_dtypes=True,
        )
        make_identity(nc, ident[:])

        for i in range(8):
            nc.vector.tensor_scalar(
                theta[:, i : i + 1], one[:], THETA ** (-i / FEAT) / (2.0 * math.pi), None, ALU.mult
            )
        nc.vector.tensor_scalar(eps[:], one[:], -1.0, EPS, ALU.add, ALU.add)
        for i in range(8, FEAT, 8):
            nc.vector.tensor_scalar(theta[:, i : i + 8], theta[:, 0:8], THETA ** (-i / FEAT), None, ALU.mult)
        shape = [P, ANGLED, FEAT]
        nc.vector.tensor_tensor(
            turns[:], pos[:].unsqueeze(2).to_broadcast(shape), theta[:].unsqueeze(1).to_broadcast(shape), ALU.mult
        )
        nc.vector.tensor_copy(whole[:], turns[:])
        nc.vector.tensor_tensor(frac[:], turns[:], whole[:], ALU.subtract)

        def first_tables():
            nc.scalar.activation(half[:], frac[:], ACT.Sin, scale=math.pi)
            nc.scalar.activation(sin[:, :ANGLED], frac[:], ACT.Sin, scale=2.0 * math.pi)
            nc.gpsimd.tensor_tensor(square[:], half[:], half[:], ALU.mult)
            nc.gpsimd.tensor_scalar(cos[:, :ANGLED], square[:], -2.0, 1.0, ALU.mult, ALU.add)

        def turn_tables(c):
            base = slice(STEPS, ANGLED)
            new = slice(STEPS + c * ROWS, STEPS + (c + 1) * ROWS)
            shape = [P, ROWS, FEAT]
            cos_by = cos[:, c - 1].unsqueeze(1).to_broadcast(shape)
            sin_by = sin[:, c - 1].unsqueeze(1).to_broadcast(shape)
            for table, a, b, op in ((cos, cos, sin, ALU.subtract), (sin, sin, cos, ALU.add)):
                left = work.tile(shape, F32, name="left", bufs=2)
                right = work.tile(shape, F32, name="right", bufs=2)
                nc.gpsimd.tensor_tensor(left[:], a[:, base], cos_by, ALU.mult)
                nc.gpsimd.tensor_tensor(right[:], b[:, base], sin_by, ALU.mult)
                nc.gpsimd.tensor_tensor(table[:, new], left[:], right[:], op)

        live = {}

        def cast(n):
            xw = work.tile([P, D], BF16, name="xw", bufs=7, align_bytes=64)
            codes = xb[:, n // J, n % J * D : (n % J + 1) * D]
            nc.scalar.copy(xw[:], codes.bitcast(FP8))
            live["xw", n] = xw

        def transpose_x(n):
            words = live.pop(("xw", n))[:].bitcast(F32)
            px = psum.tile([P, 2, G1, P], F32, name="px", bufs=2)
            for u in range(2):
                for g in range(G1):
                    nc.tensor.transpose(px[:, u, g, :], words[:, 256 * g + u : 256 * (g + 1) : 2], ident[:])
            live["px", n] = px

        def scale_x(n):
            if n % J == 0:
                live["xg", n // J] = work.tile([P, J, D // 2, 2], BF16, name="xg", align_bytes=64)
            nc.vector.tensor_tensor(
                live["xg", n // J][:, n % J].rearrange("p (g r u) e -> p g r u e", g=G1, u=2),
                live.pop(("px", n))[:].rearrange("p u g r -> p (u g r)").bitcast(BF16).rearrange(
                    "p (u g r e) -> p g r u e", u=2, g=G1, e=2
                ),
                xs[:].rearrange("p g (u e) -> p g u e", u=2).unsqueeze(2).to_broadcast([P, G1, P, 2, 2]),
                ALU.mult,
            )

        def quantize_x(k):
            xc = work.tile([P, J * G1 * P], U32, name="xc", align_bytes=64)
            xcs = work.tile([P, J * G1 * P], U8, name="xcs", align_bytes=64)
            nc.vector.quantize_mx(
                out=xc[:].bitcast(E4M3X4), scales=xcs[:], in_=live.pop(("xg", k))[:].rearrange("p j w e -> p (j w e)")
            )
            live["xc", k] = (xc, xcs)

        def matmul_x(out, n, lo, hi):
            xc, xcs = live["xc", n // J]
            for g in range(G1):
                cols = slice((n % J * G1 + g) * P, (n % J * G1 + g + 1) * P)
                nc.tensor.matmul_mx(
                    out=out,
                    lhsT=xc[:, cols].bitcast(E4M3X4),
                    lhsT_scale=xcs[:, cols],
                    rhs=wd[:, g, 2 * lo : 2 * hi].bitcast(E2M1X4),
                    rhs_scale=wds[:, g, lo:hi],
                    start=(g == 0),
                    stop=(g == G1 - 1),
                )

        def matmul_c(n):
            c = psum.tile([P, KV], F32, name="c", bufs=3)
            matmul_x(c[:], n, 0, KV)
            live["c", n] = c

        def matmul_r(k):
            r = psum.tile([P, J, ROPE], F32, name="r")
            for j in range(J):
                matmul_x(r[:, j, :], J * k + j, KV, N1)
            live["r", k] = r
            live.pop(("xc", k))

        def sum_squares(n):
            ss = work.tile([P, 1], F32, name="ss", bufs=4)
            junk = work.tile([P, KV], BF16, name="junk")
            nc.scalar.activation(junk[:], live["c", n][:], ACT.Square, accum_out=ss[:])
            live["ss", n] = ss

        def inverse_rms(n):
            rstd = work.tile([P, 1], F32, name="rstd", bufs=4)
            nc.scalar.activation(rstd[:], live.pop(("ss", n))[:], ACT.Abs_reciprocal_sqrt, bias=eps[:], scale=1.0 / KV)
            live["rstd", n] = rstd

        def make_h(n):
            h = work.tile([P, KV], BF16, name="h", bufs=4, align_bytes=64)
            nc.vector.scalar_tensor_tensor(
                h[:], live.pop(("c", n))[:], live.pop(("rstd", n))[:], gain[:], ALU.mult, ALU.mult
            )
            live["h", n] = h

        def transpose_h(n):
            if n % J == 0:
                live["ph", n // J] = psum.tile([P, 2, J, P], F32, name="ph")
            words = live.pop(("h", n))[:].bitcast(F32)
            for u in range(2):
                nc.tensor.transpose(live["ph", n // J][:, u, n % J, :], words[:, u::2], ident[:])

        def copy_h(k):
            hg = work.tile([P, J * P, 4], BF16, name="hg", align_bytes=64)
            nc.scalar.copy(
                hg[:].rearrange("p r t -> p (r t)").bitcast(F32).rearrange("p (r u) -> p r u", u=2),
                live.pop(("ph", k))[:].rearrange("p u j r -> p (j r) u"),
            )
            live["hg", k] = hg

        def quantize_h(k):
            hc = work.tile([P, J * P], U32, name="hc", align_bytes=64)
            hcs = work.tile([P, J * P], U8, name="hcs", align_bytes=64)
            nc.vector.quantize_mx(
                out=hc[:].bitcast(E4M3X4), scales=hcs[:], in_=live.pop(("hg", k))[:].rearrange("p r t -> p (r t)")
            )
            live["hc", k] = (hc, hcs)

        def matmul_kv(k):
            hc, hcs = live.pop(("hc", k))
            kv = psum.tile([P, J, N2], F32, name="kv")
            for j in range(J):
                cols = slice(j * P, (j + 1) * P)
                nc.tensor.matmul_mx(
                    out=kv[:, j, :],
                    lhsT=hc[:, cols].bitcast(E4M3X4),
                    lhsT_scale=hcs[:, cols],
                    rhs=wu[:].bitcast(E2M1X4),
                    rhs_scale=wus[:],
                    start=True,
                    stop=True,
                )
            live["kv", k] = kv

        def copy_r(k):
            rs = work.tile([P, J, 2, FEAT], F32, name="rs")
            nc.scalar.copy(rs[:].rearrange("p j d i -> p j (d i)"), live.pop(("r", k))[:])
            live["rs", k] = rs

        def rope(k):
            rows = work.tile([P, J, 6, FEAT], F32, name="rows", bufs=5)
            live["rows", k] = rows
            rs = live.pop(("rs", k))
            at = slice(STEPS + k // B * J, STEPS + (k // B + 1) * J)
            shape = [P, J, 2, FEAT]
            by_cos = work.tile([P, J, 2, FEAT], F32, name="by_cos")
            by_sin = work.tile([P, J, 2, FEAT], F32, name="by_sin")
            nc.gpsimd.tensor_tensor(by_cos[:], rs[:], cos[:, at].unsqueeze(2).to_broadcast(shape), ALU.mult)
            nc.gpsimd.tensor_tensor(by_sin[:], rs[:], sin[:, at].unsqueeze(2).to_broadcast(shape), ALU.mult)
            nc.gpsimd.tensor_tensor(rows[:, :, 1, :], by_cos[:, :, 0, :], by_sin[:, :, 1, :], ALU.subtract)
            nc.gpsimd.tensor_tensor(rows[:, :, 2, :], by_cos[:, :, 1, :], by_sin[:, :, 0, :], ALU.add)

        def copy_k(k):
            kv = live["kv", k][:].rearrange("p j (h d i) -> p j h d i", h=HEADS, d=2)
            nc.scalar.copy(live["rows", k][:, :, 0:4:3, :], kv[:, :, :, 0, :])

        def copy_v(k):
            kv = live.pop(("kv", k))[:].rearrange("p j (h d i) -> p j h d i", h=HEADS, d=2)
            rows = live.pop(("rows", k))
            nc.scalar.copy(rows[:, :, 4:6, :], kv[:, :, :, 1, :])
            rows = rows[:].rearrange("p j b i -> p j (b i)")
            at = pair_of[k]
            nc.sync.dma_start(out=kf_hbm[at, :, :, 0:256], in_=rows[:, :, 0:256])
            nc.sync.dma_start(out=kf_hbm[at, :, :, 256:384], in_=rows[:, :, 64:192])
            nc.sync.dma_start(out=v_hbm[at], in_=rows[:, :, 256:384])

        def first(stage):
            return lambda k: stage(J * k)

        def second(stage):
            return lambda k: stage(J * k + 1)

        stages = (
            (copy_r, -2),
            (first(matmul_c), -1),
            (matmul_kv, -3),
            (first(scale_x), 0),
            (first(cast), 2),
            (first(sum_squares), -1),
            (copy_k, -3),
            (first(inverse_rms), -1),
            (copy_v, -3),
            (second(make_h), -2),
            (first(transpose_x), 1),
            (second(transpose_h), -2),
            (second(matmul_c), -1),
            (matmul_r, -1),
            (second(scale_x), 0),
            (first(make_h), -1),
            (copy_h, -2),
            (second(sum_squares), -1),
            (second(cast), 2),
            (second(inverse_rms), -1),
            (second(transpose_x), 1),
            (first(transpose_h), -1),
            (quantize_x, 0),
            (quantize_h, -2),
            (rope, -2),
        )
        drain = (
            (copy_r, -1),
            (second(make_h), -1),
            (first(matmul_c), 0),
            (second(matmul_c), 0),
            (second(transpose_h), -1),
            (matmul_kv, -2),
            (matmul_r, 0),
            (first(sum_squares), 0),
            (second(sum_squares), 0),
            (first(inverse_rms), 0),
            (second(inverse_rms), 0),
            (copy_h, -1),
            (copy_k, -2),
            (copy_v, -2),
            (first(make_h), 0),
            (first(transpose_h), 0),
            (second(make_h), 0),
            (second(transpose_h), 0),
            (quantize_h, -1),
            (rope, -1),
            (copy_r, 0),
            (copy_h, 0),
            (matmul_kv, -1),
            (quantize_h, 0),
            (rope, 0),
            (copy_k, -1),
            (copy_v, -1),
            (matmul_kv, 0),
            (copy_k, 0),
            (copy_v, 0),
        )
        for step in range(-2, NPAIR):
            for stage, ahead in stages:
                if 0 <= step + ahead < NPAIR:
                    stage(step + ahead)
            if step == -1:
                first_tables()
            c = (step + 2) // 4
            if (step + 2) % 4 == 0 and 0 < c < CHUNKS:
                turn_tables(c)
        for stage, ahead in drain:
            stage(NPAIR - 1 + ahead)
